import numpy as np
import ml_dtypes


def mxq(x, axis, fmt="e4m3"):
    dtype, down = {"e4m3": (ml_dtypes.float8_e4m3fn, 7), "e5m2": (ml_dtypes.float8_e5m2, 14)}[fmt]
    v = np.moveaxis(np.asarray(x, np.float32).astype(ml_dtypes.bfloat16).astype(np.float64), axis, -1)
    blocks = v.reshape(v.shape[:-1] + (-1, 32))
    amax = np.abs(blocks).max(-1, keepdims=True)
    byte = np.maximum(np.where(amax > 0, np.frexp(amax)[1] - 1 + 127, 0) - down, 1)
    scale = np.exp2(byte - 127.0)
    codes = (blocks / scale).astype(np.float32).astype(dtype).astype(np.float64)
    return np.moveaxis((codes * scale).reshape(v.shape), -1, axis)


WIDE = False


def mx_kscale(k):
    if not WIDE:
        return np.ones(k)
    levels = np.array([10, -10, 5, -5, 0])
    a = np.random.permutation(np.resize(levels, k // 512 * 4)).reshape(k // 512, 4)
    idx = np.arange(k)
    return np.exp2(a[idx // 512, idx % 128 // 32])


BF16 = ml_dtypes.bfloat16


def bf(x):
    return np.asarray(x, np.float32).astype(BF16)


def f64(x):
    return np.asarray(x).astype(np.float64)


E2M1 = np.array([0.0, 0.5, 1.0, 1.5, 2.0, 3.0, 4.0, 6.0, -0.0, -0.5, -1.0, -1.5, -2.0, -3.0, -4.0, -6.0])


def pack_weight(w, fmt):
    k, n = w.shape
    w = f64(bf(w)).reshape(k // 32, 32, n)
    amax = np.abs(w).max(1)
    if fmt == "e4m3":
        byte = np.frexp(amax)[1] - 1 + 127 - 7
    else:
        mant, ex = np.frexp(amax / 6.0)
        byte = np.where(mant > 0.5, ex, ex - 1) + 127
    byte = np.clip(np.where(amax > 0, byte, 1), 1, 254)
    scaled = (w * np.exp2(127.0 - byte)[:, None, :]).reshape(k, n).astype(np.float32)
    by_word = np.ascontiguousarray(scaled.reshape(k // 512, 128, 4, n).transpose(0, 1, 3, 2))
    if fmt == "e4m3":
        words = by_word.astype(ml_dtypes.float8_e4m3fn).view(np.uint8)
    else:
        c = by_word.astype(ml_dtypes.float4_e2m1fn).view(np.uint8) & 0xF
        words = c[..., 0::2] | (c[..., 1::2] << 4)
    return np.ascontiguousarray(words), np.ascontiguousarray(byte.astype(np.uint8).reshape(k // 512, 16, n))


def unpack_weight(words, scales, fmt):
    g, p, n, _ = words.shape
    if fmt == "e4m3":
        vals = np.ascontiguousarray(words).view(ml_dtypes.float8_e4m3fn).astype(np.float64)
    else:
        nib = np.empty((g, p, n, 4), np.uint8)
        nib[..., 0::2] = words & 0xF
        nib[..., 1::2] = words >> 4
        vals = E2M1[nib]
    vals = vals * np.repeat(np.exp2(scales.astype(np.float64) - 127.0), 8, axis=1)[..., None]
    return vals.transpose(0, 1, 3, 2).reshape(g * 512, n)


B, NH, T, D, N, CK = 1, 6, 1024, 512, 256, 512
THETA = 2.0 ** 16


def get_freqs(n):
    q = f64(np.repeat(np.arange(0, n, 2), 2))
    return 1.0 / (THETA ** (q / n)) / (2.0 * np.pi)


def rope(phases, v):
    ph = phases * (2.0 * np.pi)
    c, s = np.cos(ph), np.sin(ph)
    even = v[..., 0::2]
    odd = v[..., 1::2]
    v_rot = np.stack((-odd, even), axis=-1).reshape(v.shape)
    return v * c + v_rot * s


def setup_inputs():
    s = mx_kscale(D)
    x = bf(np.random.standard_normal((B, 1, T, D)) * s)
    stack = np.random.standard_normal((NH, D, N)) * 0.5 / np.sqrt(D) / s[:, None]
    words, scales = pack_weight(stack.reshape(-1, N), 'e4m3')
    return {'x': x, 'encoder_words': words, 'encoder_scales': scales}


def reference(x, encoder_words, encoder_scales):
    enc = unpack_weight(encoder_words, encoder_scales, 'e4m3').reshape(NH, D, N)
    x_latent = mxq(f64(x), 3, 'e4m3') @ enc
    x_sparse = np.maximum(x_latent, 0.0)
    phases = f64(np.arange(T))[:, None] * get_freqs(N)[None, :]
    qr = rope(phases, x_sparse)
    return x_sparse, qr

@@ -1,0 +1,280 @@
+import math
+from contextlib import ExitStack
+
+import concourse.mybir as mybir
+from concourse.masks import make_identity
+
+F32 = mybir.dt.float32
+BF16 = mybir.dt.bfloat16
+I32 = mybir.dt.int32
+U32 = mybir.dt.uint32
+U8 = mybir.dt.uint8
+FP8X4 = mybir.dt.float8_e4m3fn_x4
+ALU = mybir.AluOpType
+ACT = mybir.ActivationFunctionType
+
+P = 128
+T = 1024
+D = 512
+HEADS = 6
+N = 256
+PAIRS = N // 2
+J = T // P
+HALF_J = J // 2
+BANK_J = 2
+BANK = BANK_J * N
+CHUNK = HALF_J * N
+BANKS = HALF_J // BANK_J
+WORDS = D // 2
+OCTAVES = 16
+WRAPPED = 72
+OCTAVE = 8
+AHEAD = 2
+ROUND_MAGIC = 1.5 * 2.0**23
+
+FLOPS = 2 * T * D * HEADS * N
+
+
+def tile_bdhlayer_pa_e_kernel(tc, x, encoder_words, encoder_scales, out_0, out_1):
+    nc = tc.nc
+    with ExitStack() as ctx:
+        keep = ctx.enter_context(tc.tile_pool(name="keep", bufs=1))
+        products = ctx.enter_context(tc.tile_pool(name="products", bufs=4))
+        results = ctx.enter_context(tc.tile_pool(name="results", bufs=6))
+        psum_t = ctx.enter_context(tc.psum_pool(name="psum_t", bufs=2))
+        psum_acc = ctx.enter_context(tc.psum_pool(name="psum_acc", bufs=6))
+        ctx.enter_context(tc.manual_schedule())
+
+        x_rows = x[0, 0].rearrange("(p j) k -> p j k", j=J)
+        x_sb = keep.tile([P, J, D], BF16)
+        w_words = keep.tile([P, HEADS, N], U32, align_bytes=64)
+        w_scales = keep.tile([P, HEADS, N], U8, align_bytes=64)
+
+        one = keep.tile([P, 1], F32)
+        nc.vector.memset(one[:], 1.0)
+        warm = keep.tile([P, 1], F32)
+        nc.scalar.activation(out=warm[:], in_=one[:], func=ACT.Sin)
+
+        exponent = keep.tile([P, OCTAVES], I32)
+        nc.gpsimd.iota(exponent[:], pattern=[[-1, OCTAVES]], base=127, channel_multiplier=0)
+        token_int = keep.tile([P, J], I32)
+        nc.gpsimd.iota(token_int[:], pattern=[[1, J]], base=0, channel_multiplier=J)
+        nc.gpsimd.memset(w_scales[:].rearrange("p h n -> p (h n)").bitcast(F32), 0.0)
+        identity = keep.tile([P, P], F32)
+        make_identity(nc, identity[:])
+
+        def load_x(pair):
+            pair_j = slice(pair * BANK_J, (pair + 1) * BANK_J)
+            nc.sync.dma_start(out=x_sb[:, pair_j, :], in_=x_rows[:, pair_j, :])
+
+        def load_words(first, last):
+            nc.sync.dma_start(
+                out=w_words[:, first:last, :].bitcast(I32),
+                in_=encoder_words[first:last].rearrange("h p n t -> p h (n t)").bitcast(I32),
+            )
+
+        load_x(0)
+        load_x(1)
+        load_words(0, 1)
+        for quadrant in range(4):
+            nc.sync.dma_start(
+                out=w_scales[32 * quadrant : 32 * quadrant + 4, :, :].bitcast(I32),
+                in_=encoder_scales[:, 4 * quadrant : 4 * quadrant + 4, :].rearrange("h r n -> r h n").bitcast(I32),
+            )
+        load_x(2)
+        load_x(3)
+        load_words(1, HEADS)
+
+        octave = keep.tile([P, OCTAVE], F32)
+        for r in range(OCTAVE):
+            nc.vector.tensor_scalar_mul(
+                out=octave[:, r : r + 1], in0=one[:], scalar1=2.0 ** (-r / OCTAVE) / (2.0 * math.pi)
+            )
+        halvings = keep.tile([P, OCTAVES], I32)
+        nc.vector.tensor_single_scalar(out=halvings[:], in_=exponent[:], scalar=23, op=ALU.logical_shift_left)
+        turns = keep.tile([P, OCTAVES, OCTAVE], F32)
+        nc.vector.tensor_tensor(
+            out=turns[:],
+            in0=halvings[:].bitcast(F32).unsqueeze(2).to_broadcast([P, OCTAVES, OCTAVE]),
+            in1=octave[:].unsqueeze(1).to_broadcast([P, OCTAVES, OCTAVE]),
+            op=ALU.mult,
+        )
+        token = keep.tile([P, J], F32)
+        nc.vector.tensor_copy(out=token[:], in_=token_int[:])
+
+        table_shape = [P, J, PAIRS]
+        frac = keep.tile(table_shape, F32)
+        whole = keep.tile([P, J, WRAPPED], F32)
+        half_sin = keep.tile(table_shape, F32)
+        twice_square = keep.tile(table_shape, F32)
+        cos = keep.tile(table_shape, F32)
+        sines = keep.tile([P, 2, J, PAIRS], F32)
+        grouped = keep.tile([P, J, P, 4], BF16, align_bytes=64)
+        codes = keep.tile([P, J * P], U32, align_bytes=64)
+        scales = keep.tile([P, J * P], U8, align_bytes=64)
+
+        def make_phase(js):
+            shape = [P, js.stop - js.start, PAIRS]
+            nc.vector.tensor_tensor(
+                out=frac[:, js, :],
+                in0=token[:, js].unsqueeze(2).to_broadcast(shape),
+                in1=turns[:].rearrange("p o r -> p (o r)").unsqueeze(1).to_broadcast(shape),
+                op=ALU.mult,
+            )
+
+        def make_whole(js):
+            nc.vector.tensor_scalar(
+                out=whole[:, js, :], in0=frac[:, js, 0:WRAPPED], scalar1=ROUND_MAGIC, scalar2=ROUND_MAGIC, op0=ALU.add, op1=ALU.subtract
+            )
+
+        def make_frac(js):
+            nc.vector.tensor_tensor(out=frac[:, js, 0:WRAPPED], in0=frac[:, js, 0:WRAPPED], in1=whole[:, js, :], op=ALU.subtract)
+
+        def table_steps(js):
+            return (
+                lambda: nc.scalar.activation(out=half_sin[:, js, :], in_=frac[:, js, :], func=ACT.Sin, scale=math.pi),
+                lambda: nc.scalar.activation(out=sines[:, 0, js, :], in_=frac[:, js, :], func=ACT.Sin, scale=-2.0 * math.pi),
+                lambda: nc.scalar.activation(
+                    out=twice_square[:, js, :], in_=half_sin[:, js, :], func=ACT.Square, scale=math.sqrt(2.0)
+                ),
+                lambda: nc.scalar.activation(out=sines[:, 1, js, :], in_=frac[:, js, :], func=ACT.Sin, scale=2.0 * math.pi),
+                lambda: nc.scalar.activation(out=cos[:, js, :], in_=twice_square[:, js, :], func=ACT.Copy, scale=-1.0, bias=1.0),
+            )
+
+        x_words = x_sb[:].rearrange("p j k -> p (j k)").bitcast(F32)
+        grouped_words = grouped[:].rearrange("q j t e -> q (j t e)").bitcast(F32).rearrange("q (j t u) -> q j t u", j=J, u=2)
+
+        def flip_x(pair, copy):
+            flipped = psum_t.tile([P, BANK_J, 2, P], F32, name="flipped")
+            for jj in range(BANK_J):
+                first = (pair * BANK_J + jj) * WORDS
+                for u in range(2):
+                    nc.tensor.transpose(
+                        out=flipped[:, jj, u, :], in_=x_words[:, first + u : first + WORDS : 2], identity=identity[:]
+                    )
+            copy(
+                out=grouped_words[:, pair * BANK_J : (pair + 1) * BANK_J, :, :],
+                in_=flipped[:].rearrange("q j u t -> q j t u"),
+            )
+
+        def quantise_x(first_pair, last_pair):
+            tokens = slice(first_pair * BANK_J * P, last_pair * BANK_J * P)
+            nc.vector.quantize_mx(
+                out=codes[:, tokens].bitcast(FP8X4),
+                scales=scales[:, tokens],
+                in_=grouped[:, first_pair * BANK_J : last_pair * BANK_J, :, :].rearrange("q j t e -> q (j t e)"),
+            )
+
+        pair_0, pair_1, half_1 = slice(0, 2), slice(2, 4), slice(HALF_J, J)
+        make_phase(pair_0)
+        make_phase(pair_1)
+        make_whole(pair_0)
+        make_whole(pair_1)
+        make_frac(pair_0)
+        make_frac(pair_1)
+        for step in table_steps(pair_0):
+            step()
+        make_phase(half_1)
+        flip_x(0, nc.vector.tensor_copy)
+        make_whole(half_1)
+        quantise_x(0, 1)
+        make_frac(half_1)
+        flip_x(1, nc.scalar.copy)
+        quantise_x(1, 2)
+        for step in table_steps(pair_1):
+            step()
+
+        sparse_rows = out_0[0].rearrange("h (p j) n -> h p j n", j=J)
+        rotated_rows = out_1[0].rearrange("h (p j) n -> h p j n", j=J)
+        all_banks = 2 * HEADS * BANKS
+        scalar_extras = (lambda: flip_x(2, nc.scalar.copy), lambda: flip_x(3, nc.scalar.copy)) + table_steps(half_1)
+        tiles = {}
+
+        def add(engine, chunk, columns):
+            engine.tensor_tensor(
+                out=tiles["rotated", chunk][:, columns],
+                in0=tiles["with_cos", chunk][:, columns],
+                in1=tiles["with_sin", chunk][:, columns],
+                op=ALU.add,
+            )
+
+        def store(queue, rows, kind, chunk, first_bank, last_bank):
+            half, head = divmod(chunk, HEADS)
+            nc_j = slice(half * HALF_J + first_bank * BANK_J, half * HALF_J + last_bank * BANK_J)
+            queue.dma_start(
+                out=rows[head][:, nc_j, :],
+                in_=tiles[kind, chunk][:, first_bank * BANK : last_bank * BANK].rearrange("p (j n) -> p j n", n=N),
+            )
+
+        def multiply(bank):
+            chunk, b = divmod(bank, BANKS)
+            half, head = divmod(chunk, HEADS)
+            tiles["latent", bank] = psum_acc.tile([P, BANK], F32, name="latent")
+            for jj in range(BANK_J):
+                j = half * HALF_J + b * BANK_J + jj
+                tokens = slice(j * P, (j + 1) * P)
+                nc.tensor.matmul_mx(
+                    out=tiles["latent", bank][:, jj * N : (jj + 1) * N],
+                    lhsT=codes[:, tokens].bitcast(FP8X4),
+                    lhsT_scale=scales[:, tokens],
+                    rhs=w_words[:, head, :].bitcast(FP8X4),
+                    rhs_scale=w_scales[:, head, :],
+                    start=True,
+                    stop=True,
+                )
+
+        for bank in range(AHEAD):
+            multiply(bank)
+
+        gpsimd_chunks = 2 * HEADS - 2
+        for bank in range(all_banks):
+            chunk, b = divmod(bank, BANKS)
+            half, head = divmod(chunk, HEADS)
+            if b == 0:
+                tiles["sparse", chunk] = results.tile([P, CHUNK], F32, name="sparse")
+                tiles["with_cos", chunk] = products.tile([P, CHUNK], F32, name="with_cos")
+                tiles["with_sin", chunk] = products.tile([P, CHUNK], F32, name="with_sin")
+                tiles["rotated", chunk] = results.tile([P, CHUNK], F32, name="rotated")
+            if bank == 2 * BANKS:
+                quantise_x(2, 4)
+            if bank + AHEAD < all_banks:
+                multiply(bank + AHEAD)
+
+            latent = tiles["latent", bank]
+            columns = slice(b * BANK, (b + 1) * BANK)
+            bank_j = slice(half * HALF_J + b * BANK_J, half * HALF_J + (b + 1) * BANK_J)
+            latent_pairs = latent[:].rearrange("p (q c) -> p q c", c=2)
+            nc.vector.scalar_tensor_tensor(
+                out=tiles["with_cos", chunk][:, columns].rearrange("p (q c) -> p q c", c=2),
+                in0=latent_pairs,
+                scalar=0.0,
+                in1=cos[:, bank_j, :].rearrange("p j i -> p (j i)").unsqueeze(2).to_broadcast([P, BANK // 2, 2]),
+                op0=ALU.max,
+                op1=ALU.mult,
+            )
+            nc.vector.scalar_tensor_tensor(
+                out=tiles["with_sin", chunk][:, columns].rearrange("p (q c) -> p q c", c=2),
+                in0=latent_pairs[:, :, ::-1],
+                scalar=0.0,
+                in1=sines[:, :, bank_j, :].rearrange("p c j i -> p (j i) c"),
+                op0=ALU.max,
+                op1=ALU.mult,
+            )
+            nc.scalar.activation(out=tiles["sparse", chunk][:, columns], in_=latent[:], func=ACT.Relu)
+            if chunk == 0 or chunk == 2 * HEADS - 1:
+                store(nc.scalar, sparse_rows, "sparse", chunk, b, b + 1)
+            elif b == BANKS - 1:
+                store(nc.scalar, sparse_rows, "sparse", chunk, 0, BANKS)
+            if bank < len(scalar_extras):
+                scalar_extras[bank]()
+
+            if chunk == 0:
+                add(nc.gpsimd, chunk, columns)
+                store(nc.sync, rotated_rows, "rotated", chunk, b, b + 1)
+            elif chunk < gpsimd_chunks and b == BANKS - 1:
+                add(nc.gpsimd, chunk, slice(0, CHUNK))
+                store(nc.sync, rotated_rows, "rotated", chunk, 0, BANKS)
+        for chunk in range(gpsimd_chunks, 2 * HEADS):
+            for b in range(BANKS):
+                add(nc.vector, chunk, slice(b * BANK, (b + 1) * BANK))
+                store(nc.sync, rotated_rows, "rotated", chunk, b, b + 1)

@@ -20,17 +20,17 @@ HEADS = 6
 N = 256
 PAIRS = N // 2
 J = T // P
-HALF_J = J // 2
 BANK_J = 2
 BANK = BANK_J * N
-CHUNK = HALF_J * N
-BANKS = HALF_J // BANK_J
+TOKEN_PAIRS = J // BANK_J
+BANKS = TOKEN_PAIRS * HEADS
+HALF_BANKS = BANKS // 2
+CHUNK = 2 * BANK
+CHUNKS = BANKS // 2
 WORDS = D // 2
-OCTAVES = 16
-WRAPPED = 72
-OCTAVE = 8
-AHEAD = 2
-ROUND_MAGIC = 1.5 * 2.0**23
+RATIO = 2.0 ** (-1.0 / 8.0)
+LEAD = 5
+TENSOR_CHUNKS = (3, 8)
 
 FLOPS = 2 * T * D * HEADS * N
 
@@ -39,10 +39,9 @@ def tile_bdhlayer_pa_e_kernel(tc, x, encoder_words, encoder_scales, out_0, out_1
     nc = tc.nc
     with ExitStack() as ctx:
         keep = ctx.enter_context(tc.tile_pool(name="keep", bufs=1))
-        products = ctx.enter_context(tc.tile_pool(name="products", bufs=4))
-        results = ctx.enter_context(tc.tile_pool(name="results", bufs=6))
-        psum_t = ctx.enter_context(tc.psum_pool(name="psum_t", bufs=2))
-        psum_acc = ctx.enter_context(tc.psum_pool(name="psum_acc", bufs=6))
+        products = ctx.enter_context(tc.tile_pool(name="products", bufs=5))
+        results = ctx.enter_context(tc.tile_pool(name="results", bufs=CHUNKS))
+        psum = ctx.enter_context(tc.psum_pool(name="psum", bufs=8))
         ctx.enter_context(tc.manual_schedule())
 
         x_rows = x[0, 0].rearrange("(p j) k -> p j k", j=J)
@@ -50,22 +49,24 @@ def tile_bdhlayer_pa_e_kernel(tc, x, encoder_words, encoder_scales, out_0, out_1
         w_words = keep.tile([P, HEADS, N], U32, align_bytes=64)
         w_scales = keep.tile([P, HEADS, N], U8, align_bytes=64)
 
-        one = keep.tile([P, 1], F32)
-        nc.vector.memset(one[:], 1.0)
+        ones = keep.tile([P, PAIRS], F32)
+        nc.gpsimd.memset(ones[:], 1.0)
         warm = keep.tile([P, 1], F32)
-        nc.scalar.activation(out=warm[:], in_=one[:], func=ACT.Sin)
+        nc.scalar.activation(out=warm[:], in_=ones[:, 0:1], func=ACT.Sin)
+        warm_bank = psum.tile([P, BANK], F32, name="psum_bank")
+        for part in range(3):
+            nc.tensor.matmul(
+                out=warm_bank[:, part * P : (part + 1) * P], lhsT=ones[:], rhs=ones[:], start=True, stop=True
+            )
 
-        exponent = keep.tile([P, OCTAVES], I32)
-        nc.gpsimd.iota(exponent[:], pattern=[[-1, OCTAVES]], base=127, channel_multiplier=0)
-        token_int = keep.tile([P, J], I32)
-        nc.gpsimd.iota(token_int[:], pattern=[[1, J]], base=0, channel_multiplier=J)
+        token = keep.tile([P, J], F32)
+        nc.gpsimd.iota(token[:], pattern=[[1, J]], base=0, channel_multiplier=J, allow_small_or_imprecise_dtypes=True)
         nc.gpsimd.memset(w_scales[:].rearrange("p h n -> p (h n)").bitcast(F32), 0.0)
         identity = keep.tile([P, P], F32)
         make_identity(nc, identity[:])
 
-        def load_x(pair):
-            pair_j = slice(pair * BANK_J, (pair + 1) * BANK_J)
-            nc.sync.dma_start(out=x_sb[:, pair_j, :], in_=x_rows[:, pair_j, :])
+        def load_x(js):
+            nc.sync.dma_start(out=x_sb[:, js, :], in_=x_rows[:, js, :])
 
         def load_words(first, last):
             nc.sync.dma_start(
@@ -73,148 +74,146 @@ def tile_bdhlayer_pa_e_kernel(tc, x, encoder_words, encoder_scales, out_0, out_1
                 in_=encoder_words[first:last].rearrange("h p n t -> p h (n t)").bitcast(I32),
             )
 
-        load_x(0)
-        load_x(1)
-        load_words(0, 1)
+        load_x(slice(0, 1))
+        load_x(slice(1, 2))
         for quadrant in range(4):
             nc.sync.dma_start(
                 out=w_scales[32 * quadrant : 32 * quadrant + 4, :, :].bitcast(I32),
                 in_=encoder_scales[:, 4 * quadrant : 4 * quadrant + 4, :].rearrange("h r n -> r h n").bitcast(I32),
             )
-        load_x(2)
-        load_x(3)
-        load_words(1, HEADS)
+        load_words(0, 2)
+        load_words(2, HEADS)
+        load_x(slice(2, J))
 
-        octave = keep.tile([P, OCTAVE], F32)
-        for r in range(OCTAVE):
-            nc.vector.tensor_scalar_mul(
-                out=octave[:, r : r + 1], in0=one[:], scalar1=2.0 ** (-r / OCTAVE) / (2.0 * math.pi)
-            )
-        halvings = keep.tile([P, OCTAVES], I32)
-        nc.vector.tensor_single_scalar(out=halvings[:], in_=exponent[:], scalar=23, op=ALU.logical_shift_left)
-        turns = keep.tile([P, OCTAVES, OCTAVE], F32)
-        nc.vector.tensor_tensor(
-            out=turns[:],
-            in0=halvings[:].bitcast(F32).unsqueeze(2).to_broadcast([P, OCTAVES, OCTAVE]),
-            in1=octave[:].unsqueeze(1).to_broadcast([P, OCTAVES, OCTAVE]),
-            op=ALU.mult,
+        ratio = keep.tile([P, PAIRS], F32)
+        nc.vector.tensor_scalar_mul(out=ratio[:], in0=ones[:], scalar1=RATIO)
+        turns = keep.tile([P, PAIRS], F32)
+        nc.vector.tensor_tensor_scan(
+            out=turns[:], data0=ratio[:], data1=ones[:], initial=1.0 / (2.0 * math.pi * RATIO), op0=ALU.mult, op1=ALU.min
         )
-        token = keep.tile([P, J], F32)
-        nc.vector.tensor_copy(out=token[:], in_=token_int[:])
+        quarter_turn = keep.tile([P, 1], F32)
+        nc.vector.tensor_scalar_mul(out=quarter_turn[:], in0=ones[:, 0:1], scalar1=math.pi / 2.0)
 
         table_shape = [P, J, PAIRS]
+        whole = keep.tile(table_shape, I32)
         frac = keep.tile(table_shape, F32)
-        whole = keep.tile([P, J, WRAPPED], F32)
-        half_sin = keep.tile(table_shape, F32)
-        twice_square = keep.tile(table_shape, F32)
+        distance = keep.tile(table_shape, F32)
         cos = keep.tile(table_shape, F32)
-        sines = keep.tile([P, 2, J, PAIRS], F32)
+        sines = [keep.tile([P, 2, BANK_J, PAIRS], F32, name="sines_" + str(pair)) for pair in range(TOKEN_PAIRS)]
         grouped = keep.tile([P, J, P, 4], BF16, align_bytes=64)
         codes = keep.tile([P, J * P], U32, align_bytes=64)
         scales = keep.tile([P, J * P], U8, align_bytes=64)
 
-        def make_phase(js):
-            shape = [P, js.stop - js.start, PAIRS]
-            nc.vector.tensor_tensor(
-                out=frac[:, js, :],
-                in0=token[:, js].unsqueeze(2).to_broadcast(shape),
-                in1=turns[:].rearrange("p o r -> p (o r)").unsqueeze(1).to_broadcast(shape),
-                op=ALU.mult,
+        def make_whole(j):
+            nc.vector.tensor_scalar(out=whole[:, j, :], in0=turns[:], scalar1=token[:, j : j + 1], scalar2=None, op0=ALU.mult)
+
+        def make_frac(j):
+            nc.vector.scalar_tensor_tensor(
+                out=frac[:, j, :], in0=turns[:], scalar=token[:, j : j + 1], in1=whole[:, j, :], op0=ALU.mult, op1=ALU.subtract
             )
 
-        def make_whole(js):
-            nc.vector.tensor_scalar(
-                out=whole[:, js, :], in0=frac[:, js, 0:WRAPPED], scalar1=ROUND_MAGIC, scalar2=ROUND_MAGIC, op0=ALU.add, op1=ALU.subtract
-            )
+        def tokens_of(pair):
+            return slice(pair * BANK_J, (pair + 1) * BANK_J)
 
-        def make_frac(js):
-            nc.vector.tensor_tensor(out=frac[:, js, 0:WRAPPED], in0=frac[:, js, 0:WRAPPED], in1=whole[:, js, :], op=ALU.subtract)
-
-        def table_steps(js):
+        def table_steps(pair):
+            js = tokens_of(pair)
             return (
-                lambda: nc.scalar.activation(out=half_sin[:, js, :], in_=frac[:, js, :], func=ACT.Sin, scale=math.pi),
-                lambda: nc.scalar.activation(out=sines[:, 0, js, :], in_=frac[:, js, :], func=ACT.Sin, scale=-2.0 * math.pi),
+                lambda: nc.scalar.activation(out=distance[:, js, :], in_=frac[:, js, :], func=ACT.Abs),
+                lambda: nc.scalar.activation(out=sines[pair][:, 0, :, :], in_=frac[:, js, :], func=ACT.Sin, scale=-2.0 * math.pi),
                 lambda: nc.scalar.activation(
-                    out=twice_square[:, js, :], in_=half_sin[:, js, :], func=ACT.Square, scale=math.sqrt(2.0)
+                    out=cos[:, js, :], in_=distance[:, js, :], func=ACT.Sin, scale=-2.0 * math.pi, bias=quarter_turn[:]
                 ),
-                lambda: nc.scalar.activation(out=sines[:, 1, js, :], in_=frac[:, js, :], func=ACT.Sin, scale=2.0 * math.pi),
-                lambda: nc.scalar.activation(out=cos[:, js, :], in_=twice_square[:, js, :], func=ACT.Copy, scale=-1.0, bias=1.0),
+                lambda: nc.scalar.activation(out=sines[pair][:, 1, :, :], in_=frac[:, js, :], func=ACT.Sin, scale=2.0 * math.pi),
             )
 
         x_words = x_sb[:].rearrange("p j k -> p (j k)").bitcast(F32)
         grouped_words = grouped[:].rearrange("q j t e -> q (j t e)").bitcast(F32).rearrange("q (j t u) -> q j t u", j=J, u=2)
 
-        def flip_x(pair, copy):
-            flipped = psum_t.tile([P, BANK_J, 2, P], F32, name="flipped")
-            for jj in range(BANK_J):
-                first = (pair * BANK_J + jj) * WORDS
+        def flip_x(js, copy):
+            flipped = psum.tile([P, BANK_J, 2, P], F32, name="psum_bank")
+            for jj, j in enumerate(range(js.start, js.stop)):
                 for u in range(2):
                     nc.tensor.transpose(
-                        out=flipped[:, jj, u, :], in_=x_words[:, first + u : first + WORDS : 2], identity=identity[:]
+                        out=flipped[:, jj, u, :],
+                        in_=x_words[:, j * WORDS + u : (j + 1) * WORDS : 2],
+                        identity=identity[:],
                     )
             copy(
-                out=grouped_words[:, pair * BANK_J : (pair + 1) * BANK_J, :, :],
-                in_=flipped[:].rearrange("q j u t -> q j t u"),
+                out=grouped_words[:, js, :, :],
+                in_=flipped[:, 0 : js.stop - js.start, :, :].rearrange("q j u t -> q j t u"),
             )
 
-        def quantise_x(first_pair, last_pair):
-            tokens = slice(first_pair * BANK_J * P, last_pair * BANK_J * P)
+        def quantise_x(js):
+            tokens = slice(js.start * P, js.stop * P)
             nc.vector.quantize_mx(
                 out=codes[:, tokens].bitcast(FP8X4),
                 scales=scales[:, tokens],
-                in_=grouped[:, first_pair * BANK_J : last_pair * BANK_J, :, :].rearrange("q j t e -> q (j t e)"),
+                in_=grouped[:, js, :, :].rearrange("q j t e -> q (j t e)"),
             )
 
-        pair_0, pair_1, half_1 = slice(0, 2), slice(2, 4), slice(HALF_J, J)
-        make_phase(pair_0)
-        make_phase(pair_1)
-        make_whole(pair_0)
-        make_whole(pair_1)
-        make_frac(pair_0)
-        make_frac(pair_1)
-        for step in table_steps(pair_0):
-            step()
-        make_phase(half_1)
-        flip_x(0, nc.vector.tensor_copy)
-        make_whole(half_1)
-        quantise_x(0, 1)
-        make_frac(half_1)
-        flip_x(1, nc.scalar.copy)
-        quantise_x(1, 2)
-        for step in table_steps(pair_1):
+        for j in range(6):
+            make_whole(j)
+        for pair in range(3):
+            for j in range(2 * pair, 2 * pair + 2):
+                make_frac(j)
+            if pair == 0:
+                for step in table_steps(0):
+                    step()
+        make_whole(6)
+        make_whole(7)
+        flip_x(slice(0, 1), nc.vector.tensor_copy)
+        flip_x(slice(1, 2), nc.scalar.copy)
+        quantise_x(slice(0, 1))
+        quantise_x(slice(1, 2))
+        make_frac(6)
+        make_frac(7)
+        for step in table_steps(1):
             step()
 
-        sparse_rows = out_0[0].rearrange("h (p j) n -> h p j n", j=J)
-        rotated_rows = out_1[0].rearrange("h (p j) n -> h p j n", j=J)
-        all_banks = 2 * HEADS * BANKS
-        scalar_extras = (lambda: flip_x(2, nc.scalar.copy), lambda: flip_x(3, nc.scalar.copy)) + table_steps(half_1)
+        all_rows = {"sparse": out_0[0], "rotated": out_1[0]}
         tiles = {}
 
-        def add(engine, chunk, columns):
-            engine.tensor_tensor(
-                out=tiles["rotated", chunk][:, columns],
-                in0=tiles["with_cos", chunk][:, columns],
-                in1=tiles["with_sin", chunk][:, columns],
-                op=ALU.add,
+        def head_and_pair(bank):
+            if bank < HALF_BANKS:
+                return bank % HEADS, bank // HEADS
+            return (bank - HALF_BANKS) // 2, 2 + bank % 2
+
+        def result(kind, chunk):
+            if (kind, chunk) not in tiles:
+                tiles[kind, chunk] = results.tile([P, CHUNK], F32, name=kind)
+            return tiles[kind, chunk]
+
+        def in_chunk(bank):
+            return slice(bank % 2 * BANK, (bank % 2 + 1) * BANK)
+
+        def store_bank(kind, bank):
+            head, pair = head_and_pair(bank)
+            nc.sync.dma_start(
+                out=all_rows[kind][head].rearrange("(p j) n -> p j n", j=J)[:, tokens_of(pair), :],
+                in_=result(kind, bank // 2)[:, in_chunk(bank)].rearrange("p (j n) -> p j n", n=N),
             )
 
-        def store(queue, rows, kind, chunk, first_bank, last_bank):
-            half, head = divmod(chunk, HEADS)
-            nc_j = slice(half * HALF_J + first_bank * BANK_J, half * HALF_J + last_bank * BANK_J)
-            queue.dma_start(
-                out=rows[head][:, nc_j, :],
-                in_=tiles[kind, chunk][:, first_bank * BANK : last_bank * BANK].rearrange("p (j n) -> p j n", n=N),
-            )
+        def store_chunk(kind, chunk):
+            head, pair = head_and_pair(2 * chunk)
+            if 2 * chunk < HALF_BANKS:
+                nc.sync.dma_start(
+                    out=all_rows[kind][head : head + 2].rearrange("h (p j) n -> p h j n", j=J)[:, :, tokens_of(pair), :],
+                    in_=result(kind, chunk)[:].rearrange("p (h j n) -> p h j n", h=2, n=N),
+                )
+            else:
+                nc.sync.dma_start(
+                    out=all_rows[kind][head].rearrange("(p j) n -> p j n", j=J)[:, J // 2 : J, :],
+                    in_=result(kind, chunk)[:].rearrange("p (j n) -> p j n", n=N),
+                )
 
         def multiply(bank):
-            chunk, b = divmod(bank, BANKS)
-            half, head = divmod(chunk, HEADS)
-            tiles["latent", bank] = psum_acc.tile([P, BANK], F32, name="latent")
+            head, pair = head_and_pair(bank)
+            latent = psum.tile([P, BANK], F32, name="psum_bank")
             for jj in range(BANK_J):
-                j = half * HALF_J + b * BANK_J + jj
+                j = pair * BANK_J + jj
                 tokens = slice(j * P, (j + 1) * P)
                 nc.tensor.matmul_mx(
-                    out=tiles["latent", bank][:, jj * N : (jj + 1) * N],
+                    out=latent[:, jj * N : (jj + 1) * N],
                     lhsT=codes[:, tokens].bitcast(FP8X4),
                     lhsT_scale=scales[:, tokens],
                     rhs=w_words[:, head, :].bitcast(FP8X4),
@@ -222,59 +221,123 @@ def tile_bdhlayer_pa_e_kernel(tc, x, encoder_words, encoder_scales, out_0, out_1
                     start=True,
                     stop=True,
                 )
+            return latent
 
-        for bank in range(AHEAD):
-            multiply(bank)
+        def relu(bank, latent):
+            nc.scalar.activation(out=result("sparse", bank // 2)[:, in_chunk(bank)], in_=latent[:], func=ACT.Relu)
+            if bank < 8:
+                store_bank("sparse", bank)
+            elif bank % 2 == 1:
+                store_chunk("sparse", bank // 2)
 
-        gpsimd_chunks = 2 * HEADS - 2
-        for bank in range(all_banks):
-            chunk, b = divmod(bank, BANKS)
-            half, head = divmod(chunk, HEADS)
-            if b == 0:
-                tiles["sparse", chunk] = results.tile([P, CHUNK], F32, name="sparse")
+        def add(engine, chunk, columns):
+            engine.tensor_tensor(
+                out=result("rotated", chunk)[:, columns],
+                in0=tiles["with_cos", chunk][:, columns],
+                in1=tiles["with_sin", chunk][:, columns],
+                op=ALU.add,
+            )
+
+        def tensor_add(bank):
+            tiles["sum", bank] = psum.tile([P, BANK], F32, name="psum_bank")
+            for kind in ("with_cos", "with_sin"):
+                nc.tensor.matmul(
+                    out=tiles["sum", bank][:],
+                    lhsT=identity[:],
+                    rhs=tiles[kind, bank // 2][:, in_chunk(bank)],
+                    start=kind == "with_cos",
+                    stop=kind == "with_sin",
+                )
+
+        def take_sum(bank):
+            nc.scalar.copy(out=result("rotated", bank // 2)[:, in_chunk(bank)], in_=tiles["sum", bank][:])
+            store_bank("rotated", bank)
+
+        def next_bank(bank):
+            tiles["latent", bank] = multiply(bank)
+            relu(bank, tiles["latent", bank])
+
+        first_for_scalar = []
+        for bank in range(2):
+            tiles["latent", bank] = multiply(bank)
+            first_for_scalar.append(multiply(bank))
+        for bank in range(2):
+            relu(bank, first_for_scalar[bank])
+        next_bank(2)
+
+        late_tables = table_steps(2) + table_steps(3)
+        for bank in range(BANKS):
+            chunk = bank // 2
+            if bank % 2 == 0:
                 tiles["with_cos", chunk] = products.tile([P, CHUNK], F32, name="with_cos")
                 tiles["with_sin", chunk] = products.tile([P, CHUNK], F32, name="with_sin")
-                tiles["rotated", chunk] = results.tile([P, CHUNK], F32, name="rotated")
-            if bank == 2 * BANKS:
-                quantise_x(2, 4)
-            if bank + AHEAD < all_banks:
-                multiply(bank + AHEAD)
+            if bank == 4:
+                for ahead in range(8, 4 + LEAD):
+                    next_bank(ahead)
+            if bank >= 4 and bank + LEAD < BANKS:
+                next_bank(bank + LEAD)
+            if 4 <= bank < 8:
+                late_tables[2 * (bank - 4)]()
+                late_tables[2 * (bank - 4) + 1]()
 
-            latent = tiles["latent", bank]
-            columns = slice(b * BANK, (b + 1) * BANK)
-            bank_j = slice(half * HALF_J + b * BANK_J, half * HALF_J + (b + 1) * BANK_J)
-            latent_pairs = latent[:].rearrange("p (q c) -> p q c", c=2)
+            head, pair = head_and_pair(bank)
+            latent_pairs = tiles["latent", bank][:].rearrange("p (q c) -> p q c", c=2)
             nc.vector.scalar_tensor_tensor(
-                out=tiles["with_cos", chunk][:, columns].rearrange("p (q c) -> p q c", c=2),
+                out=tiles["with_cos", chunk][:, in_chunk(bank)].rearrange("p (q c) -> p q c", c=2),
                 in0=latent_pairs,
                 scalar=0.0,
-                in1=cos[:, bank_j, :].rearrange("p j i -> p (j i)").unsqueeze(2).to_broadcast([P, BANK // 2, 2]),
+                in1=cos[:, tokens_of(pair), :].rearrange("p j i -> p (j i)").unsqueeze(2).to_broadcast([P, BANK // 2, 2]),
                 op0=ALU.max,
                 op1=ALU.mult,
             )
+            if bank == 3:
+                quantise_x(tokens_of(1))
+                next_bank(6)
+                next_bank(7)
+            if bank == 4:
+                quantise_x(slice(4, J))
             nc.vector.scalar_tensor_tensor(
-                out=tiles["with_sin", chunk][:, columns].rearrange("p (q c) -> p q c", c=2),
+                out=tiles["with_sin", chunk][:, in_chunk(bank)].rearrange("p (q c) -> p q c", c=2),
                 in0=latent_pairs[:, :, ::-1],
                 scalar=0.0,
-                in1=sines[:, :, bank_j, :].rearrange("p c j i -> p (j i) c"),
+                in1=sines[pair][:].rearrange("p c j i -> p (j i) c"),
                 op0=ALU.max,
                 op1=ALU.mult,
             )
-            nc.scalar.activation(out=tiles["sparse", chunk][:, columns], in_=latent[:], func=ACT.Relu)
-            if chunk == 0 or chunk == 2 * HEADS - 1:
-                store(nc.scalar, sparse_rows, "sparse", chunk, b, b + 1)
-            elif b == BANKS - 1:
-                store(nc.scalar, sparse_rows, "sparse", chunk, 0, BANKS)
-            if bank < len(scalar_extras):
-                scalar_extras[bank]()
 
             if chunk == 0:
-                add(nc.gpsimd, chunk, columns)
-                store(nc.sync, rotated_rows, "rotated", chunk, b, b + 1)
-            elif chunk < gpsimd_chunks and b == BANKS - 1:
+                add(nc.gpsimd, chunk, in_chunk(bank))
+            if bank == 0:
+                next_bank(3)
+                flip_x(tokens_of(1), nc.scalar.copy)
+            if bank == 1:
+                store_bank("rotated", 0)
+                next_bank(4)
+                flip_x(tokens_of(2), nc.scalar.copy)
+                flip_x(tokens_of(3), nc.scalar.copy)
+            if bank == 2:
+                store_bank("rotated", 1)
+                next_bank(5)
+            if bank == 4:
+                add(nc.gpsimd, 2, in_chunk(4))
+                add(nc.gpsimd, 1, slice(0, CHUNK))
+            if bank == 5:
+                store_bank("rotated", 4)
+                add(nc.gpsimd, 2, in_chunk(5))
+            if bank == 7:
+                store_chunk("rotated", 1)
+                store_bank("rotated", 5)
+            if bank % 2 == 1 and 3 <= chunk < CHUNKS - 1 and chunk not in TENSOR_CHUNKS:
                 add(nc.gpsimd, chunk, slice(0, CHUNK))
-                store(nc.sync, rotated_rows, "rotated", chunk, 0, BANKS)
-        for chunk in range(gpsimd_chunks, 2 * HEADS):
-            for b in range(BANKS):
-                add(nc.vector, chunk, slice(b * BANK, (b + 1) * BANK))
-                store(nc.sync, rotated_rows, "rotated", chunk, b, b + 1)
+            for tensor_chunk in TENSOR_CHUNKS:
+                for b in range(2):
+                    if bank == 2 * tensor_chunk + 2 + 2 * b:
+                        tensor_add(2 * tensor_chunk + b)
+                    if bank == 2 * tensor_chunk + 4 + 2 * b:
+                        take_sum(2 * tensor_chunk + b)
+            if bank % 2 == 1 and chunk >= 5 and chunk - 2 not in TENSOR_CHUNKS:
+                store_chunk("rotated", chunk - 2)
+        store_chunk("rotated", CHUNKS - 2)
+        for bank in range(BANKS - 2, BANKS):
+            add(nc.vector, CHUNKS - 1, in_chunk(bank))
+            store_bank("rotated", bank)

@@ -171,6 +171,7 @@ def tile_bdhlayer_pa_e_kernel(tc, x, encoder_words, encoder_scales, out_0, out_1
             step()
 
         all_rows = {"sparse": out_0[0], "rotated": out_1[0]}
+        queues = {"sparse": nc.scalar, "rotated": nc.sync}
         tiles = {}
 
         def head_and_pair(bank):
@@ -188,7 +189,7 @@ def tile_bdhlayer_pa_e_kernel(tc, x, encoder_words, encoder_scales, out_0, out_1
 
         def store_bank(kind, bank):
             head, pair = head_and_pair(bank)
-            nc.sync.dma_start(
+            queues[kind].dma_start(
                 out=all_rows[kind][head].rearrange("(p j) n -> p j n", j=J)[:, tokens_of(pair), :],
                 in_=result(kind, bank // 2)[:, in_chunk(bank)].rearrange("p (j n) -> p j n", n=N),
             )
@@ -196,12 +197,12 @@ def tile_bdhlayer_pa_e_kernel(tc, x, encoder_words, encoder_scales, out_0, out_1
         def store_chunk(kind, chunk):
             head, pair = head_and_pair(2 * chunk)
             if 2 * chunk < HALF_BANKS:
-                nc.sync.dma_start(
+                queues[kind].dma_start(
                     out=all_rows[kind][head : head + 2].rearrange("h (p j) n -> p h j n", j=J)[:, :, tokens_of(pair), :],
                     in_=result(kind, chunk)[:].rearrange("p (h j n) -> p h j n", h=2, n=N),
                 )
             else:
-                nc.sync.dma_start(
+                queues[kind].dma_start(
                     out=all_rows[kind][head].rearrange("(p j) n -> p j n", j=J)[:, J // 2 : J, :],
                     in_=result(kind, chunk)[:].rearrange("p (j n) -> p j n", n=N),
                 )
@@ -225,9 +226,11 @@ def tile_bdhlayer_pa_e_kernel(tc, x, encoder_words, encoder_scales, out_0, out_1
 
         def relu(bank, latent):
             nc.scalar.activation(out=result("sparse", bank // 2)[:, in_chunk(bank)], in_=latent[:], func=ACT.Relu)
-            if bank < 8:
-                store_bank("sparse", bank)
-            elif bank % 2 == 1:
+            if 1 <= bank < 9:
+                store_bank("sparse", bank - 1)
+            elif bank % 2 == 0 and bank > 0:
+                store_chunk("sparse", bank // 2 - 1)
+            elif bank == BANKS - 1:
                 store_chunk("sparse", bank // 2)
 
         def add(engine, chunk, columns):

@@ -29,6 +29,7 @@ CHUNK = 2 * BANK
 CHUNKS = BANKS // 2
 WORDS = D // 2
 RATIO = 2.0 ** (-1.0 / 8.0)
+FINE_CHUNK = 9
 LEAD = 5
 TENSOR_CHUNKS = (3, 8)
 
@@ -187,9 +188,9 @@ def tile_bdhlayer_pa_e_kernel(tc, x, encoder_words, encoder_scales, out_0, out_1
         def in_chunk(bank):
             return slice(bank % 2 * BANK, (bank % 2 + 1) * BANK)
 
-        def store_bank(kind, bank):
+        def store_bank(kind, bank, queue=None):
             head, pair = head_and_pair(bank)
-            queues[kind].dma_start(
+            (queue or queues[kind]).dma_start(
                 out=all_rows[kind][head].rearrange("(p j) n -> p j n", j=J)[:, tokens_of(pair), :],
                 in_=result(kind, bank // 2)[:, in_chunk(bank)].rearrange("p (j n) -> p j n", n=N),
             )
@@ -226,9 +227,11 @@ def tile_bdhlayer_pa_e_kernel(tc, x, encoder_words, encoder_scales, out_0, out_1
 
         def relu(bank, latent):
             nc.scalar.activation(out=result("sparse", bank // 2)[:, in_chunk(bank)], in_=latent[:], func=ACT.Relu)
-            if 1 <= bank < 9:
+            if bank < 6:
+                store_bank("sparse", bank, nc.sync)
+            elif 7 <= bank < 9:
                 store_bank("sparse", bank - 1)
-            elif bank % 2 == 0 and bank > 0:
+            elif bank % 2 == 0 and bank > 8:
                 store_chunk("sparse", bank // 2 - 1)
             elif bank == BANKS - 1:
                 store_chunk("sparse", bank // 2)
@@ -330,17 +333,21 @@ def tile_bdhlayer_pa_e_kernel(tc, x, encoder_words, encoder_scales, out_0, out_1
             if bank == 7:
                 store_chunk("rotated", 1)
                 store_bank("rotated", 5)
-            if bank % 2 == 1 and 3 <= chunk < CHUNKS - 1 and chunk not in TENSOR_CHUNKS:
-                add(nc.gpsimd, chunk, slice(0, CHUNK))
+            if 3 <= chunk < CHUNKS - 1 and chunk not in TENSOR_CHUNKS:
+                if chunk >= FINE_CHUNK:
+                    add(nc.gpsimd, chunk, in_chunk(bank))
+                elif bank % 2 == 1:
+                    add(nc.gpsimd, chunk, slice(0, CHUNK))
             for tensor_chunk in TENSOR_CHUNKS:
                 for b in range(2):
                     if bank == 2 * tensor_chunk + 2 + 2 * b:
                         tensor_add(2 * tensor_chunk + b)
                     if bank == 2 * tensor_chunk + 4 + 2 * b:
                         take_sum(2 * tensor_chunk + b)
-            if bank % 2 == 1 and chunk >= 5 and chunk - 2 not in TENSOR_CHUNKS:
-                store_chunk("rotated", chunk - 2)
-        store_chunk("rotated", CHUNKS - 2)
+            if bank % 2 == 1 and 3 <= chunk - 1 < FINE_CHUNK and chunk - 1 not in TENSOR_CHUNKS:
+                store_chunk("rotated", chunk - 1)
+            if bank - 2 >= 2 * FINE_CHUNK:
+                store_bank("rotated", bank - 2)
         for bank in range(BANKS - 2, BANKS):
             add(nc.vector, CHUNKS - 1, in_chunk(bank))
             store_bank("rotated", bank)

@@ -257,34 +257,32 @@ def tile_bdhlayer_pa_e_kernel(tc, x, encoder_words, encoder_scales, out_0, out_1
 
         def take_sum(bank):
             nc.scalar.copy(out=result("rotated", bank // 2)[:, in_chunk(bank)], in_=tiles["sum", bank][:])
-            store_bank("rotated", bank)
+            store_bank("rotated", bank, nc.scalar)
 
         def next_bank(bank):
             tiles["latent", bank] = multiply(bank)
             relu(bank, tiles["latent", bank])
 
-        first_for_scalar = []
-        for bank in range(2):
-            tiles["latent", bank] = multiply(bank)
-            first_for_scalar.append(multiply(bank))
-        for bank in range(2):
-            relu(bank, first_for_scalar[bank])
+        tiles["latent", 0] = multiply(0)
+        next_bank(1)
         next_bank(2)
 
-        late_tables = table_steps(2) + table_steps(3)
+        late_tables = table_steps(3)
         for bank in range(BANKS):
             chunk = bank // 2
             if bank % 2 == 0:
                 tiles["with_cos", chunk] = products.tile([P, CHUNK], F32, name="with_cos")
                 tiles["with_sin", chunk] = products.tile([P, CHUNK], F32, name="with_sin")
-            if bank == 4:
-                for ahead in range(8, 4 + LEAD):
+            if bank == 5:
+                for ahead in range(8, 5 + LEAD):
                     next_bank(ahead)
-            if bank >= 4 and bank + LEAD < BANKS:
+            if bank >= 5 and bank + LEAD < BANKS:
                 next_bank(bank + LEAD)
-            if 4 <= bank < 8:
-                late_tables[2 * (bank - 4)]()
-                late_tables[2 * (bank - 4) + 1]()
+            if bank == 4:
+                for step in table_steps(2):
+                    step()
+            if 6 <= bank < 10:
+                late_tables[bank - 6]()
 
             head, pair = head_and_pair(bank)
             latent_pairs = tiles["latent", bank][:].rearrange("p (q c) -> p q c", c=2)
@@ -296,11 +294,11 @@ def tile_bdhlayer_pa_e_kernel(tc, x, encoder_words, encoder_scales, out_0, out_1
                 op0=ALU.max,
                 op1=ALU.mult,
             )
-            if bank == 3:
+            if bank == 4:
                 quantise_x(tokens_of(1))
                 next_bank(6)
                 next_bank(7)
-            if bank == 4:
+            if bank == 5:
                 quantise_x(slice(4, J))
             nc.vector.scalar_tensor_tensor(
                 out=tiles["with_sin", chunk][:, in_chunk(bank)].rearrange("p (q c) -> p q c", c=2),
@@ -311,28 +309,20 @@ def tile_bdhlayer_pa_e_kernel(tc, x, encoder_words, encoder_scales, out_0, out_1
                 op1=ALU.mult,
             )
 
-            if chunk == 0:
-                add(nc.gpsimd, chunk, in_chunk(bank))
+            for added in {0: (0,), 1: (1,), 2: (2,), 5: (5, 3, 4)}.get(bank, ()):
+                add(nc.gpsimd, added // 2, in_chunk(added))
+            for stored in {1: (0,), 2: (1,), 4: (2,), 7: (5,), 8: (3, 4)}.get(bank, ()):
+                store_bank("rotated", stored)
             if bank == 0:
+                relu(0, tiles["latent", 0])
                 next_bank(3)
                 flip_x(tokens_of(1), nc.scalar.copy)
             if bank == 1:
-                store_bank("rotated", 0)
                 next_bank(4)
                 flip_x(tokens_of(2), nc.scalar.copy)
                 flip_x(tokens_of(3), nc.scalar.copy)
             if bank == 2:
-                store_bank("rotated", 1)
                 next_bank(5)
-            if bank == 4:
-                add(nc.gpsimd, 2, in_chunk(4))
-                add(nc.gpsimd, 1, slice(0, CHUNK))
-            if bank == 5:
-                store_bank("rotated", 4)
-                add(nc.gpsimd, 2, in_chunk(5))
-            if bank == 7:
-                store_chunk("rotated", 1)
-                store_bank("rotated", 5)
             if 3 <= chunk < CHUNKS - 1 and chunk not in TENSOR_CHUNKS:
                 if chunk >= FINE_CHUNK:
                     add(nc.gpsimd, chunk, in_chunk(bank))
@@ -348,6 +338,6 @@ def tile_bdhlayer_pa_e_kernel(tc, x, encoder_words, encoder_scales, out_0, out_1
                 store_chunk("rotated", chunk - 1)
             if bank - 2 >= 2 * FINE_CHUNK:
                 store_bank("rotated", bank - 2)
-        for bank in range(BANKS - 2, BANKS):
+        for bank, queue in ((BANKS - 2, nc.scalar), (BANKS - 1, nc.sync)):
             add(nc.vector, CHUNKS - 1, in_chunk(bank))
-            store_bank("rotated", bank)
+            store_bank("rotated", bank, queue)

@@ -24,14 +24,13 @@ BANK_J = 2
 BANK = BANK_J * N
 TOKEN_PAIRS = J // BANK_J
 BANKS = TOKEN_PAIRS * HEADS
-HALF_BANKS = BANKS // 2
-CHUNK = 2 * BANK
-CHUNKS = BANKS // 2
+GROUP = 3
+GROUPS = BANKS // GROUP
+FIRST = HEADS
 WORDS = D // 2
 RATIO = 2.0 ** (-1.0 / 8.0)
-FINE_CHUNK = 9
+TENSOR_BANKS = (7, 12, 15, 19)
 LEAD = 5
-TENSOR_CHUNKS = (3, 8)
 
 FLOPS = 2 * T * D * HEADS * N
 
@@ -40,8 +39,8 @@ def tile_bdhlayer_pa_e_kernel(tc, x, encoder_words, encoder_scales, out_0, out_1
     nc = tc.nc
     with ExitStack() as ctx:
         keep = ctx.enter_context(tc.tile_pool(name="keep", bufs=1))
-        products = ctx.enter_context(tc.tile_pool(name="products", bufs=5))
-        results = ctx.enter_context(tc.tile_pool(name="results", bufs=CHUNKS))
+        products = ctx.enter_context(tc.tile_pool(name="products", bufs=4))
+        results = ctx.enter_context(tc.tile_pool(name="results", bufs=GROUPS))
         psum = ctx.enter_context(tc.psum_pool(name="psum", bufs=8))
         ctx.enter_context(tc.manual_schedule())
 
@@ -172,75 +171,73 @@ def tile_bdhlayer_pa_e_kernel(tc, x, encoder_words, encoder_scales, out_0, out_1
             step()
 
         all_rows = {"sparse": out_0[0], "rotated": out_1[0]}
-        queues = {"sparse": nc.scalar, "rotated": nc.sync}
         tiles = {}
 
         def head_and_pair(bank):
-            if bank < HALF_BANKS:
-                return bank % HEADS, bank // HEADS
-            return (bank - HALF_BANKS) // 2, 2 + bank % 2
+            if bank < 6:
+                return bank, 0
+            if bank < 8:
+                return bank - 6, 1
+            if bank < 12:
+                return (bank - 8) // 2, 2 + bank % 2
+            return bank // GROUP - 2, 1 + bank % GROUP
 
-        def result(kind, chunk):
-            if (kind, chunk) not in tiles:
-                tiles[kind, chunk] = results.tile([P, CHUNK], F32, name=kind)
-            return tiles[kind, chunk]
-
-        def in_chunk(bank):
-            return slice(bank % 2 * BANK, (bank % 2 + 1) * BANK)
-
-        def store_bank(kind, bank, queue=None):
+        def group_of(bank):
             head, pair = head_and_pair(bank)
-            (queue or queues[kind]).dma_start(
-                out=all_rows[kind][head].rearrange("(p j) n -> p j n", j=J)[:, tokens_of(pair), :],
-                in_=result(kind, bank // 2)[:, in_chunk(bank)].rearrange("p (j n) -> p j n", n=N),
+            return head // GROUP if pair == 0 else 2 + head
+
+        def result(kind, group):
+            if (kind, group) not in tiles:
+                tiles[kind, group] = results.tile([P, GROUP * BANK], F32, name=kind)
+            return tiles[kind, group]
+
+        def in_group(bank):
+            head, pair = head_and_pair(bank)
+            place = head % GROUP if pair == 0 else pair - 1
+            return slice(place * BANK, (place + 1) * BANK)
+
+        def store(queue, kind, first, last):
+            head, pair = head_and_pair(first)
+            queue.dma_start(
+                out=all_rows[kind][head].rearrange("(p j) n -> p j n", j=J)[:, pair * BANK_J : (pair + last - first) * BANK_J, :],
+                in_=result(kind, group_of(first))[:, in_group(first).start : in_group(last - 1).stop].rearrange("p (j n) -> p j n", n=N),
             )
 
-        def store_chunk(kind, chunk):
-            head, pair = head_and_pair(2 * chunk)
-            if 2 * chunk < HALF_BANKS:
-                queues[kind].dma_start(
-                    out=all_rows[kind][head : head + 2].rearrange("h (p j) n -> p h j n", j=J)[:, :, tokens_of(pair), :],
-                    in_=result(kind, chunk)[:].rearrange("p (h j n) -> p h j n", h=2, n=N),
-                )
-            else:
-                queues[kind].dma_start(
-                    out=all_rows[kind][head].rearrange("(p j) n -> p j n", j=J)[:, J // 2 : J, :],
-                    in_=result(kind, chunk)[:].rearrange("p (j n) -> p j n", n=N),
-                )
+        def multiply_token(out, head, j):
+            tokens = slice(j * P, (j + 1) * P)
+            nc.tensor.matmul_mx(
+                out=out,
+                lhsT=codes[:, tokens].bitcast(FP8X4),
+                lhsT_scale=scales[:, tokens],
+                rhs=w_words[:, head, :].bitcast(FP8X4),
+                rhs_scale=w_scales[:, head, :],
+                start=True,
+                stop=True,
+            )
 
         def multiply(bank):
             head, pair = head_and_pair(bank)
             latent = psum.tile([P, BANK], F32, name="psum_bank")
             for jj in range(BANK_J):
-                j = pair * BANK_J + jj
-                tokens = slice(j * P, (j + 1) * P)
-                nc.tensor.matmul_mx(
-                    out=latent[:, jj * N : (jj + 1) * N],
-                    lhsT=codes[:, tokens].bitcast(FP8X4),
-                    lhsT_scale=scales[:, tokens],
-                    rhs=w_words[:, head, :].bitcast(FP8X4),
-                    rhs_scale=w_scales[:, head, :],
-                    start=True,
-                    stop=True,
-                )
+                multiply_token(latent[:, jj * N : (jj + 1) * N], head, pair * BANK_J + jj)
             return latent
 
         def relu(bank, latent):
-            nc.scalar.activation(out=result("sparse", bank // 2)[:, in_chunk(bank)], in_=latent[:], func=ACT.Relu)
-            if bank < 6:
-                store_bank("sparse", bank, nc.sync)
-            elif 7 <= bank < 9:
-                store_bank("sparse", bank - 1)
-            elif bank % 2 == 0 and bank > 8:
-                store_chunk("sparse", bank // 2 - 1)
-            elif bank == BANKS - 1:
-                store_chunk("sparse", bank // 2)
+            nc.scalar.activation(out=result("sparse", group_of(bank))[:, in_group(bank)], in_=latent[:], func=ACT.Relu)
+            if bank < 8:
+                store(nc.sync, "sparse", bank, bank + 1)
+            elif bank < 12:
+                if bank % 2 == 1:
+                    store(nc.scalar, "sparse", bank - 1, bank + 1)
+            elif bank % GROUP == GROUP - 1:
+                store(nc.scalar, "sparse", bank - GROUP + 1, bank + 1)
 
-        def add(engine, chunk, columns):
+        def add(engine, first, last):
+            columns = slice(in_group(first).start, in_group(last - 1).stop)
             engine.tensor_tensor(
-                out=result("rotated", chunk)[:, columns],
-                in0=tiles["with_cos", chunk][:, columns],
-                in1=tiles["with_sin", chunk][:, columns],
+                out=result("rotated", group_of(first))[:, columns],
+                in0=tiles["with_cos", group_of(first)][:, columns],
+                in1=tiles["with_sin", group_of(first)][:, columns],
                 op=ALU.add,
             )
 
@@ -250,14 +247,13 @@ def tile_bdhlayer_pa_e_kernel(tc, x, encoder_words, encoder_scales, out_0, out_1
                 nc.tensor.matmul(
                     out=tiles["sum", bank][:],
                     lhsT=identity[:],
-                    rhs=tiles[kind, bank // 2][:, in_chunk(bank)],
+                    rhs=tiles[kind, group_of(bank)][:, in_group(bank)],
                     start=kind == "with_cos",
                     stop=kind == "with_sin",
                 )
 
         def take_sum(bank):
-            nc.scalar.copy(out=result("rotated", bank // 2)[:, in_chunk(bank)], in_=tiles["sum", bank][:])
-            store_bank("rotated", bank, nc.scalar)
+            nc.scalar.copy(out=result("rotated", group_of(bank))[:, in_group(bank)], in_=tiles["sum", bank][:])
 
         def next_bank(bank):
             tiles["latent", bank] = multiply(bank)
@@ -267,27 +263,25 @@ def tile_bdhlayer_pa_e_kernel(tc, x, encoder_words, encoder_scales, out_0, out_1
         next_bank(1)
         next_bank(2)
 
-        late_tables = table_steps(3)
+        late_tables = table_steps(2) + table_steps(3)
         for bank in range(BANKS):
-            chunk = bank // 2
-            if bank % 2 == 0:
-                tiles["with_cos", chunk] = products.tile([P, CHUNK], F32, name="with_cos")
-                tiles["with_sin", chunk] = products.tile([P, CHUNK], F32, name="with_sin")
-            if bank == 5:
-                for ahead in range(8, 5 + LEAD):
-                    next_bank(ahead)
-            if bank >= 5 and bank + LEAD < BANKS:
-                next_bank(bank + LEAD)
+            group = group_of(bank)
+            if ("with_cos", group) not in tiles:
+                tiles["with_cos", group] = products.tile([P, GROUP * BANK], F32, name="with_cos")
+                tiles["with_sin", group] = products.tile([P, GROUP * BANK], F32, name="with_sin")
             if bank == 4:
-                for step in table_steps(2):
-                    step()
-            if 6 <= bank < 10:
-                late_tables[bank - 6]()
+                late_tables[0]()
+                late_tables[1]()
+            if bank == 6:
+                for ahead in range(9, 6 + LEAD):
+                    next_bank(ahead)
+            if bank > 5 and bank + LEAD < BANKS:
+                next_bank(bank + LEAD)
 
             head, pair = head_and_pair(bank)
             latent_pairs = tiles["latent", bank][:].rearrange("p (q c) -> p q c", c=2)
             nc.vector.scalar_tensor_tensor(
-                out=tiles["with_cos", chunk][:, in_chunk(bank)].rearrange("p (q c) -> p q c", c=2),
+                out=tiles["with_cos", group][:, in_group(bank)].rearrange("p (q c) -> p q c", c=2),
                 in0=latent_pairs,
                 scalar=0.0,
                 in1=cos[:, tokens_of(pair), :].rearrange("p j i -> p (j i)").unsqueeze(2).to_broadcast([P, BANK // 2, 2]),
@@ -298,10 +292,15 @@ def tile_bdhlayer_pa_e_kernel(tc, x, encoder_words, encoder_scales, out_0, out_1
                 quantise_x(tokens_of(1))
                 next_bank(6)
                 next_bank(7)
+                late_tables[2]()
+                late_tables[3]()
             if bank == 5:
                 quantise_x(slice(4, J))
+                next_bank(8)
+                for step in late_tables[4:]:
+                    step()
             nc.vector.scalar_tensor_tensor(
-                out=tiles["with_sin", chunk][:, in_chunk(bank)].rearrange("p (q c) -> p q c", c=2),
+                out=tiles["with_sin", group][:, in_group(bank)].rearrange("p (q c) -> p q c", c=2),
                 in0=latent_pairs[:, :, ::-1],
                 scalar=0.0,
                 in1=sines[pair][:].rearrange("p c j i -> p (j i) c"),
@@ -310,9 +309,9 @@ def tile_bdhlayer_pa_e_kernel(tc, x, encoder_words, encoder_scales, out_0, out_1
             )
 
             for added in {0: (0,), 1: (1,), 2: (2,), 5: (5, 3, 4)}.get(bank, ()):
-                add(nc.gpsimd, added // 2, in_chunk(added))
-            for stored in {1: (0,), 2: (1,), 4: (2,), 7: (5,), 8: (3, 4)}.get(bank, ()):
-                store_bank("rotated", stored)
+                add(nc.gpsimd, added, added + 1)
+            for stored in {1: (0,), 2: (1,), 4: (2,), 7: (5,), 8: (3, 4), 9: (6,)}.get(bank, ()):
+                store(nc.sync, "rotated", stored, stored + 1)
             if bank == 0:
                 relu(0, tiles["latent", 0])
                 next_bank(3)
@@ -323,21 +322,33 @@ def tile_bdhlayer_pa_e_kernel(tc, x, encoder_words, encoder_scales, out_0, out_1
                 flip_x(tokens_of(3), nc.scalar.copy)
             if bank == 2:
                 next_bank(5)
-            if 3 <= chunk < CHUNKS - 1 and chunk not in TENSOR_CHUNKS:
-                if chunk >= FINE_CHUNK:
-                    add(nc.gpsimd, chunk, in_chunk(bank))
-                elif bank % 2 == 1:
-                    add(nc.gpsimd, chunk, slice(0, CHUNK))
-            for tensor_chunk in TENSOR_CHUNKS:
-                for b in range(2):
-                    if bank == 2 * tensor_chunk + 2 + 2 * b:
-                        tensor_add(2 * tensor_chunk + b)
-                    if bank == 2 * tensor_chunk + 4 + 2 * b:
-                        take_sum(2 * tensor_chunk + b)
-            if bank % 2 == 1 and 3 <= chunk - 1 < FINE_CHUNK and chunk - 1 not in TENSOR_CHUNKS:
-                store_chunk("rotated", chunk - 1)
-            if bank - 2 >= 2 * FINE_CHUNK:
-                store_bank("rotated", bank - 2)
+            if bank in (6, 7) and bank not in TENSOR_BANKS:
+                add(nc.gpsimd, bank, bank + 1)
+            if bank in (9, 11):
+                add(nc.gpsimd, bank - 1, bank + 1)
+            if 12 <= bank < 18 and bank % GROUP == GROUP - 1:
+                add(nc.gpsimd, bank - 1 if bank - 2 in TENSOR_BANKS else bank - 2, bank + 1)
+            if 18 <= bank < BANKS - 2 and bank not in TENSOR_BANKS:
+                add(nc.gpsimd, bank, bank + 1)
+            if bank - 2 in TENSOR_BANKS:
+                tensor_add(bank - 2)
+            if bank - 4 in TENSOR_BANKS:
+                take_sum(bank - 4)
+                if bank - 4 < 12:
+                    store(nc.scalar, "rotated", bank - 4, bank - 4 + 1)
+            if bank - 2 in (9, 11):
+                store(nc.sync, "rotated", bank - 2 - 1, bank - 2 + 1)
+            done = bank - 2
+            if bank == 20:
+                store(nc.sync, "rotated", 18, 19)
+            if 12 <= done < 18 and done % GROUP == GROUP - 1:
+                store(nc.sync, "rotated", done - GROUP + 1, done + 1)
+        for bank in TENSOR_BANKS:
+            if bank + 4 >= BANKS:
+                take_sum(bank)
+        store(nc.scalar, "rotated", 19, 21)
+        for bank in range(BANKS - GROUP, BANKS - 2):
+            store(nc.sync, "rotated", bank, bank + 1)
         for bank, queue in ((BANKS - 2, nc.scalar), (BANKS - 1, nc.sync)):
-            add(nc.vector, CHUNKS - 1, in_chunk(bank))
-            store_bank("rotated", bank, queue)
+            add(nc.vector, bank, bank + 1)
+            store(queue, "rotated", bank, bank + 1)

import math
from contextlib import ExitStack

import concourse.mybir as mybir
from concourse.masks import make_identity

F32 = mybir.dt.float32
BF16 = mybir.dt.bfloat16
I32 = mybir.dt.int32
U32 = mybir.dt.uint32
U8 = mybir.dt.uint8
FP8X4 = mybir.dt.float8_e4m3fn_x4
ALU = mybir.AluOpType
ACT = mybir.ActivationFunctionType

P = 128
T = 1024
D = 512
HEADS = 6
N = 256
PAIRS = N // 2
J = T // P
BANK_J = 2
BANK = BANK_J * N
TOKEN_PAIRS = J // BANK_J
BANKS = TOKEN_PAIRS * HEADS
GROUP = 3
GROUPS = BANKS // GROUP
FIRST = HEADS
WORDS = D // 2
RATIO = 2.0 ** (-1.0 / 8.0)
TENSOR_BANKS = (7, 12, 15, 19)
LEAD = 5

FLOPS = 2 * T * D * HEADS * N


def tile_bdhlayer_pa_e_kernel(tc, x, encoder_words, encoder_scales, out_0, out_1):
    nc = tc.nc
    with ExitStack() as ctx:
        keep = ctx.enter_context(tc.tile_pool(name="keep", bufs=1))
        products = ctx.enter_context(tc.tile_pool(name="products", bufs=4))
        results = ctx.enter_context(tc.tile_pool(name="results", bufs=GROUPS))
        psum = ctx.enter_context(tc.psum_pool(name="psum", bufs=8))
        ctx.enter_context(tc.manual_schedule())

        x_rows = x[0, 0].rearrange("(p j) k -> p j k", j=J)
        x_sb = keep.tile([P, J, D], BF16)
        w_words = keep.tile([P, HEADS, N], U32, align_bytes=64)
        w_scales = keep.tile([P, HEADS, N], U8, align_bytes=64)

        ones = keep.tile([P, PAIRS], F32)
        nc.gpsimd.memset(ones[:], 1.0)
        warm = keep.tile([P, 1], F32)
        nc.scalar.activation(out=warm[:], in_=ones[:, 0:1], func=ACT.Sin)
        warm_bank = psum.tile([P, BANK], F32, name="psum_bank")
        for part in range(3):
            nc.tensor.matmul(
                out=warm_bank[:, part * P : (part + 1) * P], lhsT=ones[:], rhs=ones[:], start=True, stop=True
            )

        token = keep.tile([P, J], F32)
        nc.gpsimd.iota(token[:], pattern=[[1, J]], base=0, channel_multiplier=J, allow_small_or_imprecise_dtypes=True)
        nc.gpsimd.memset(w_scales[:].rearrange("p h n -> p (h n)").bitcast(F32), 0.0)
        identity = keep.tile([P, P], F32)
        make_identity(nc, identity[:])

        def load_x(js):
            nc.sync.dma_start(out=x_sb[:, js, :], in_=x_rows[:, js, :])

        def load_words(first, last):
            nc.sync.dma_start(
                out=w_words[:, first:last, :].bitcast(I32),
                in_=encoder_words[first:last].rearrange("h p n t -> p h (n t)").bitcast(I32),
            )

        load_x(slice(0, 1))
        load_x(slice(1, 2))
        for quadrant in range(4):
            nc.sync.dma_start(
                out=w_scales[32 * quadrant : 32 * quadrant + 4, :, :].bitcast(I32),
                in_=encoder_scales[:, 4 * quadrant : 4 * quadrant + 4, :].rearrange("h r n -> r h n").bitcast(I32),
            )
        load_words(0, 2)
        load_words(2, HEADS)
        load_x(slice(2, J))

        ratio = keep.tile([P, PAIRS], F32)
        nc.vector.tensor_scalar_mul(out=ratio[:], in0=ones[:], scalar1=RATIO)
        turns = keep.tile([P, PAIRS], F32)
        nc.vector.tensor_tensor_scan(
            out=turns[:], data0=ratio[:], data1=ones[:], initial=1.0 / (2.0 * math.pi * RATIO), op0=ALU.mult, op1=ALU.min
        )
        quarter_turn = keep.tile([P, 1], F32)
        nc.vector.tensor_scalar_mul(out=quarter_turn[:], in0=ones[:, 0:1], scalar1=math.pi / 2.0)

        table_shape = [P, J, PAIRS]
        whole = keep.tile(table_shape, I32)
        frac = keep.tile(table_shape, F32)
        distance = keep.tile(table_shape, F32)
        cos = keep.tile(table_shape, F32)
        sines = [keep.tile([P, 2, BANK_J, PAIRS], F32, name="sines_" + str(pair)) for pair in range(TOKEN_PAIRS)]
        grouped = keep.tile([P, J, P, 4], BF16, align_bytes=64)
        codes = keep.tile([P, J * P], U32, align_bytes=64)
        scales = keep.tile([P, J * P], U8, align_bytes=64)

        def make_whole(j):
            nc.vector.tensor_scalar(out=whole[:, j, :], in0=turns[:], scalar1=token[:, j : j + 1], scalar2=None, op0=ALU.mult)

        def make_frac(j):
            nc.vector.scalar_tensor_tensor(
                out=frac[:, j, :], in0=turns[:], scalar=token[:, j : j + 1], in1=whole[:, j, :], op0=ALU.mult, op1=ALU.subtract
            )

        def tokens_of(pair):
            return slice(pair * BANK_J, (pair + 1) * BANK_J)

        def table_steps(pair):
            js = tokens_of(pair)
            return (
                lambda: nc.scalar.activation(out=distance[:, js, :], in_=frac[:, js, :], func=ACT.Abs),
                lambda: nc.scalar.activation(out=sines[pair][:, 0, :, :], in_=frac[:, js, :], func=ACT.Sin, scale=-2.0 * math.pi),
                lambda: nc.scalar.activation(
                    out=cos[:, js, :], in_=distance[:, js, :], func=ACT.Sin, scale=-2.0 * math.pi, bias=quarter_turn[:]
                ),
                lambda: nc.scalar.activation(out=sines[pair][:, 1, :, :], in_=frac[:, js, :], func=ACT.Sin, scale=2.0 * math.pi),
            )

        x_words = x_sb[:].rearrange("p j k -> p (j k)").bitcast(F32)
        grouped_words = grouped[:].rearrange("q j t e -> q (j t e)").bitcast(F32).rearrange("q (j t u) -> q j t u", j=J, u=2)

        def flip_x(js, copy):
            flipped = psum.tile([P, BANK_J, 2, P], F32, name="psum_bank")
            for jj, j in enumerate(range(js.start, js.stop)):
                for u in range(2):
                    nc.tensor.transpose(
                        out=flipped[:, jj, u, :],
                        in_=x_words[:, j * WORDS + u : (j + 1) * WORDS : 2],
                        identity=identity[:],
                    )
            copy(
                out=grouped_words[:, js, :, :],
                in_=flipped[:, 0 : js.stop - js.start, :, :].rearrange("q j u t -> q j t u"),
            )

        def quantise_x(js):
            tokens = slice(js.start * P, js.stop * P)
            nc.vector.quantize_mx(
                out=codes[:, tokens].bitcast(FP8X4),
                scales=scales[:, tokens],
                in_=grouped[:, js, :, :].rearrange("q j t e -> q (j t e)"),
            )

        for j in range(6):
            make_whole(j)
        for pair in range(3):
            for j in range(2 * pair, 2 * pair + 2):
                make_frac(j)
            if pair == 0:
                for step in table_steps(0):
                    step()
        make_whole(6)
        make_whole(7)
        flip_x(slice(0, 1), nc.vector.tensor_copy)
        flip_x(slice(1, 2), nc.scalar.copy)
        quantise_x(slice(0, 1))
        quantise_x(slice(1, 2))
        make_frac(6)
        make_frac(7)
        for step in table_steps(1):
            step()

        all_rows = {"sparse": out_0[0], "rotated": out_1[0]}
        tiles = {}

        def head_and_pair(bank):
            if bank < 6:
                return bank, 0
            if bank < 8:
                return bank - 6, 1
            if bank < 12:
                return (bank - 8) // 2, 2 + bank % 2
            return bank // GROUP - 2, 1 + bank % GROUP

        def group_of(bank):
            head, pair = head_and_pair(bank)
            return head // GROUP if pair == 0 else 2 + head

        def result(kind, group):
            if (kind, group) not in tiles:
                tiles[kind, group] = results.tile([P, GROUP * BANK], F32, name=kind)
            return tiles[kind, group]

        def in_group(bank):
            head, pair = head_and_pair(bank)
            place = head % GROUP if pair == 0 else pair - 1
            return slice(place * BANK, (place + 1) * BANK)

        def store(queue, kind, first, last):
            head, pair = head_and_pair(first)
            queue.dma_start(
                out=all_rows[kind][head].rearrange("(p j) n -> p j n", j=J)[:, pair * BANK_J : (pair + last - first) * BANK_J, :],
                in_=result(kind, group_of(first))[:, in_group(first).start : in_group(last - 1).stop].rearrange("p (j n) -> p j n", n=N),
            )

        def multiply_token(out, head, j):
            tokens = slice(j * P, (j + 1) * P)
            nc.tensor.matmul_mx(
                out=out,
                lhsT=codes[:, tokens].bitcast(FP8X4),
                lhsT_scale=scales[:, tokens],
                rhs=w_words[:, head, :].bitcast(FP8X4),
                rhs_scale=w_scales[:, head, :],
                start=True,
                stop=True,
            )

        def multiply(bank):
            head, pair = head_and_pair(bank)
            latent = psum.tile([P, BANK], F32, name="psum_bank")
            for jj in range(BANK_J):
                multiply_token(latent[:, jj * N : (jj + 1) * N], head, pair * BANK_J + jj)
            return latent

        def relu(bank, latent):
            nc.scalar.activation(out=result("sparse", group_of(bank))[:, in_group(bank)], in_=latent[:], func=ACT.Relu)
            if bank < 8:
                store(nc.sync, "sparse", bank, bank + 1)
            elif bank < 12:
                if bank % 2 == 1:
                    store(nc.scalar, "sparse", bank - 1, bank + 1)
            elif bank % GROUP == GROUP - 1:
                store(nc.scalar, "sparse", bank - GROUP + 1, bank + 1)

        def add(engine, first, last):
            columns = slice(in_group(first).start, in_group(last - 1).stop)
            engine.tensor_tensor(
                out=result("rotated", group_of(first))[:, columns],
                in0=tiles["with_cos", group_of(first)][:, columns],
                in1=tiles["with_sin", group_of(first)][:, columns],
                op=ALU.add,
            )

        def tensor_add(bank):
            tiles["sum", bank] = psum.tile([P, BANK], F32, name="psum_bank")
            for kind in ("with_cos", "with_sin"):
                nc.tensor.matmul(
                    out=tiles["sum", bank][:],
                    lhsT=identity[:],
                    rhs=tiles[kind, group_of(bank)][:, in_group(bank)],
                    start=kind == "with_cos",
                    stop=kind == "with_sin",
                )

        def take_sum(bank):
            nc.scalar.copy(out=result("rotated", group_of(bank))[:, in_group(bank)], in_=tiles["sum", bank][:])

        def next_bank(bank):
            tiles["latent", bank] = multiply(bank)
            relu(bank, tiles["latent", bank])

        tiles["latent", 0] = multiply(0)
        next_bank(1)
        next_bank(2)

        late_tables = table_steps(2) + table_steps(3)
        for bank in range(BANKS):
            group = group_of(bank)
            if ("with_cos", group) not in tiles:
                tiles["with_cos", group] = products.tile([P, GROUP * BANK], F32, name="with_cos")
                tiles["with_sin", group] = products.tile([P, GROUP * BANK], F32, name="with_sin")
            if bank == 4:
                late_tables[0]()
                late_tables[1]()
            if bank == 6:
                for ahead in range(9, 6 + LEAD):
                    next_bank(ahead)
            if bank > 5 and bank + LEAD < BANKS:
                next_bank(bank + LEAD)

            head, pair = head_and_pair(bank)
            latent_pairs = tiles["latent", bank][:].rearrange("p (q c) -> p q c", c=2)
            nc.vector.scalar_tensor_tensor(
                out=tiles["with_cos", group][:, in_group(bank)].rearrange("p (q c) -> p q c", c=2),
                in0=latent_pairs,
                scalar=0.0,
                in1=cos[:, tokens_of(pair), :].rearrange("p j i -> p (j i)").unsqueeze(2).to_broadcast([P, BANK // 2, 2]),
                op0=ALU.max,
                op1=ALU.mult,
            )
            if bank == 4:
                quantise_x(tokens_of(1))
                next_bank(6)
                next_bank(7)
                late_tables[2]()
                late_tables[3]()
            if bank == 5:
                quantise_x(slice(4, J))
                next_bank(8)
                for step in late_tables[4:]:
                    step()
            nc.vector.scalar_tensor_tensor(
                out=tiles["with_sin", group][:, in_group(bank)].rearrange("p (q c) -> p q c", c=2),
                in0=latent_pairs[:, :, ::-1],
                scalar=0.0,
                in1=sines[pair][:].rearrange("p c j i -> p (j i) c"),
                op0=ALU.max,
                op1=ALU.mult,
            )

            for added in {0: (0,), 1: (1,), 2: (2,), 5: (5, 3, 4)}.get(bank, ()):
                add(nc.gpsimd, added, added + 1)
            for stored in {1: (0,), 2: (1,), 4: (2,), 7: (5,), 8: (3, 4), 9: (6,)}.get(bank, ()):
                store(nc.sync, "rotated", stored, stored + 1)
            if bank == 0:
                relu(0, tiles["latent", 0])
                next_bank(3)
                flip_x(tokens_of(1), nc.scalar.copy)
            if bank == 1:
                next_bank(4)
                flip_x(tokens_of(2), nc.scalar.copy)
                flip_x(tokens_of(3), nc.scalar.copy)
            if bank == 2:
                next_bank(5)
            if bank in (6, 7) and bank not in TENSOR_BANKS:
                add(nc.gpsimd, bank, bank + 1)
            if bank in (9, 11):
                add(nc.gpsimd, bank - 1, bank + 1)
            if 12 <= bank < 18 and bank % GROUP == GROUP - 1:
                add(nc.gpsimd, bank - 1 if bank - 2 in TENSOR_BANKS else bank - 2, bank + 1)
            if 18 <= bank < BANKS - 2 and bank not in TENSOR_BANKS:
                add(nc.gpsimd, bank, bank + 1)
            if bank - 2 in TENSOR_BANKS:
                tensor_add(bank - 2)
            if bank - 4 in TENSOR_BANKS:
                take_sum(bank - 4)
                if bank - 4 < 12:
                    store(nc.scalar, "rotated", bank - 4, bank - 4 + 1)
            if bank - 2 in (9, 11):
                store(nc.sync, "rotated", bank - 2 - 1, bank - 2 + 1)
            done = bank - 2
            if bank == 20:
                store(nc.sync, "rotated", 18, 19)
            if 12 <= done < 18 and done % GROUP == GROUP - 1:
                store(nc.sync, "rotated", done - GROUP + 1, done + 1)
        for bank in TENSOR_BANKS:
            if bank + 4 >= BANKS:
                take_sum(bank)
        store(nc.scalar, "rotated", 19, 21)
        for bank in range(BANKS - GROUP, BANKS - 2):
            store(nc.sync, "rotated", bank, bank + 1)
        for bank, queue in ((BANKS - 2, nc.scalar), (BANKS - 1, nc.sync)):
            add(nc.vector, bank, bank + 1)
            store(queue, "rotated", bank, bank + 1)
